import numpy as np
import ml_dtypes


def mxq(x, axis, fmt="e4m3"):
    dtype, down = {"e4m3": (ml_dtypes.float8_e4m3fn, 7), "e5m2": (ml_dtypes.float8_e5m2, 14)}[fmt]
    v = np.moveaxis(np.asarray(x, np.float32).astype(ml_dtypes.bfloat16).astype(np.float64), axis, -1)
    blocks = v.reshape(v.shape[:-1] + (-1, 32))
    amax = np.abs(blocks).max(-1, keepdims=True)
    byte = np.maximum(np.where(amax > 0, np.frexp(amax)[1] - 1 + 127, 0) - down, 1)
    scale = np.exp2(byte - 127.0)
    codes = (blocks / scale).astype(np.float32).astype(dtype).astype(np.float64)
    return np.moveaxis((codes * scale).reshape(v.shape), -1, axis)


WIDE = False


def mx_kscale(k):
    if not WIDE:
        return np.ones(k)
    levels = np.array([10, -10, 5, -5, 0])
    if k % 512:
        return np.exp2(np.random.permutation(np.resize(levels, k // 32))).repeat(32)
    a = np.empty((k // 512, 16))
    for p in range(k // 512):
        a[p, :8] = np.random.permutation(np.resize(levels, 8))
        for g in range(8):
            far = levels[np.abs(levels - a[p, g]) >= 10]
            a[p, g + 8] = far[np.random.randint(len(far))]
    return np.exp2(a.ravel()).repeat(32)


BF16 = ml_dtypes.bfloat16


def bf(x):
    return np.asarray(x, np.float32).astype(BF16)


def f64(x):
    return np.asarray(x).astype(np.float64)


B, S, D, H, KV, DH, W, KB = 4, 2048, 1024, 1, 1, 128, 128, 512
THETA = 10000.0


def rotate_half(t):
    half = t.shape[-1] // 2
    return np.concatenate((-t[..., half:], t[..., :half]), axis=-1)


def rope_cos_sin():
    inv_freq = 1.0 / THETA ** (np.arange(0, DH, 2) / DH)
    ang = np.arange(S)[:, None] * inv_freq[None, :]
    cos = np.repeat(np.cos(ang), 2, axis=-1)[None, :, None, :]
    sin = np.repeat(np.sin(ang), 2, axis=-1)[None, :, None, :]
    return cos, sin


def setup_inputs():
    s = mx_kscale(D)
    return {"x": bf(np.random.standard_normal((B, S, D)) * s),
            "Wq": bf(np.random.standard_normal((D, H * DH)) / np.sqrt(D) / s[:, None]),
            "Wk": bf(np.random.standard_normal((D, KV * DH)) / np.sqrt(D) / s[:, None]),
            "Wv": bf(np.random.standard_normal((D, KV * DH)) * 1.5 / np.sqrt(D) / s[:, None])}


def reference(x, Wq, Wk, Wv):
    cos, sin = rope_cos_sin()
    xq = mxq(f64(x), 2, "e4m3")
    q = (xq @ mxq(f64(Wq), 0, "e4m3")).reshape(B, S, H, DH)
    k = (xq @ mxq(f64(Wk), 0, "e4m3")).reshape(B, S, KV, DH)
    v = (xq @ mxq(f64(Wv), 0, "e4m3")).reshape(B, S, KV, DH)
    q = q * cos + rotate_half(q) * sin
    k = k * cos + rotate_half(k) * sin
    return q.transpose(0, 2, 1, 3), k.transpose(0, 2, 1, 3), v.transpose(0, 2, 1, 3)

@@ -1,0 +1,327 @@
+import math
+from contextlib import ExitStack
+
+import concourse.mybir as mybir
+from concourse.masks import make_identity
+
+F32 = mybir.dt.float32
+BF16 = mybir.dt.bfloat16
+I32 = mybir.dt.int32
+U32 = mybir.dt.uint32
+U8 = mybir.dt.uint8
+FP8X4 = mybir.dt.float8_e4m3fn_x4
+ALU = mybir.AluOpType
+ACT = mybir.ActivationFunctionType
+
+B, S, D, DH = 4, 2048, 1024, 128
+THETA = 10000.0
+P = 128
+J = S // P
+JN = 4
+NCH = B * J // JN
+NP = NCH * JN // 2
+LEAD = 8
+NB = 10
+HALF = DH // 2
+NF = DH // 2
+NSEED = 8
+
+FLOPS = 2 * B * S * D * 3 * DH
+
+
+def tile_spikinggroupedslidingattention_pa_t_kernel(tc, x, Wq, Wk, Wv, out_0, out_1, out_2):
+    nc = tc.nc
+    chunks = [(jc, b) for jc in range(J // JN) for b in range(B)]
+    with ExitStack() as ctx:
+        const = ctx.enter_context(tc.tile_pool(name="const", bufs=1))
+        xin = ctx.enter_context(tc.tile_pool(name="xin", bufs=NB))
+        grp = ctx.enter_context(tc.tile_pool(name="grp", bufs=4))
+        cod = ctx.enter_context(tc.tile_pool(name="cod", bufs=3))
+        prod = ctx.enter_context(tc.tile_pool(name="prod", bufs=3))
+        outp = ctx.enter_context(tc.tile_pool(name="outp", bufs=4))
+        tb = ctx.enter_context(tc.tile_pool(name="tb", bufs=1))
+        ps_t = ctx.enter_context(tc.psum_pool(name="ps_t", bufs=4))
+        ps_q = ctx.enter_context(tc.psum_pool(name="ps_q", bufs=2))
+        ps_v = ctx.enter_context(tc.psum_pool(name="ps_v", bufs=2))
+
+        xcs = {}
+        xts = {}
+        grs = {}
+        cods = {}
+        accs = {}
+        oqks = {}
+        pts = {}
+        ovs = {}
+
+        def load_part(c, lo, hi):
+            jc, b = chunks[c]
+            nc.sync.dma_start(
+                out=xcs[c][:, lo * D : hi * D].rearrange("p (j d) -> p j d", j=hi - lo),
+                in_=x[b].rearrange("(p j) d -> p j d", j=J)[:, jc * JN + lo : jc * JN + hi, :],
+            )
+
+        def load(c):
+            xc = xin.tile([P, JN * D], BF16)
+            xcs[c] = xc
+            if c > 0:
+                load_part(c, 0, JN)
+
+        wraw = const.tile([P, 3, 2, 4, DH], BF16)
+        load(0)
+        load_part(0, 0, 1)
+        for wi, w_dram in enumerate((Wq, Wk, Wv)):
+            nc.sync.dma_start(
+                out=wraw[:, wi].rearrange("p g t n -> p g (t n)"),
+                in_=w_dram.rearrange("(g p t) n -> p g (t n)", g=2, p=P, t=4),
+            )
+        load_part(0, 1, 2)
+        load_part(0, 2, JN)
+        for c in range(1, LEAD):
+            load(c)
+
+        ident = const.tile([P, P], F32)
+        make_identity(nc, ident[:])
+        pos_i = const.tile([P, J], I32)
+        nc.gpsimd.iota(pos_i[:], pattern=[[1, J]], base=0, channel_multiplier=J)
+
+        ones = const.tile([P, NSEED], F32)
+        nc.vector.memset(ones[:], 1.0)
+        warm = const.tile([P, 1], F32)
+        nc.scalar.activation(out=warm[:], in_=ones[:, 0:1], func=ACT.Sin)
+        fq = const.tile([P, NF], F32)
+        for m in range(NSEED):
+            nc.vector.tensor_scalar_mul(
+                out=fq[:, m : m + 1], in0=ones[:, m : m + 1], scalar1=THETA ** (-m / NF) / (2.0 * math.pi)
+            )
+        n_have = NSEED
+        while n_have < NF:
+            nc.vector.tensor_scalar_mul(
+                out=fq[:, n_have : 2 * n_have], in0=fq[:, 0:n_have], scalar1=THETA ** (-n_have / NF)
+            )
+            n_have *= 2
+        pos = const.tile([P, J], F32)
+        nc.vector.tensor_copy(out=pos[:], in_=pos_i[:])
+
+        cos_t = const.tile([P, J, DH], F32)
+        sin_t = const.tile([P, J, DH], F32)
+        tabs = {}
+        raws = {}
+        halves = {}
+        squares = {}
+
+        def table_turns(jc):
+            turns = tb.tile([P, JN, NF], F32)
+            for jj in range(JN):
+                j = jc * JN + jj
+                nc.scalar.activation(out=turns[:, jj, :], in_=fq[:], func=ACT.Copy, scale=pos[:, j : j + 1])
+            whole = tb.tile([P, JN, NF], U32)
+            nc.scalar.copy(out=whole[:], in_=turns[:])
+            raws[jc] = (turns, whole)
+
+        def table_vector(jc):
+            turns, whole = raws[jc]
+            frac = tb.tile([P, JN, NF], F32)
+            nc.vector.tensor_tensor(out=frac[:], in0=turns[:], in1=whole[:].bitcast(I32), op=ALU.subtract)
+            tabs[jc] = frac
+
+        def table_scalar(jc, part):
+            js = slice(jc * JN, (jc + 1) * JN)
+            frac = tabs[jc]
+            if part == 0:
+                hs = tb.tile([P, JN, NF], F32)
+                nc.scalar.activation(out=hs[:], in_=frac[:], func=ACT.Sin, scale=math.pi)
+                halves[jc] = hs
+            elif part == 1:
+                sq = tb.tile([P, JN, NF], F32)
+                nc.scalar.activation(out=sq[:], in_=halves[jc][:], func=ACT.Square)
+                squares[jc] = sq
+            elif part == 2:
+                nc.scalar.activation(
+                    out=cos_t[:, js, :].rearrange("p j (m e) -> p j m e", e=2),
+                    in_=squares[jc][:].unsqueeze(3).to_broadcast([P, JN, NF, 2]),
+                    func=ACT.Copy,
+                    bias=1.0,
+                    scale=-2.0,
+                )
+            elif part == 3:
+                nc.scalar.activation(
+                    out=sin_t[:, js, 0:HALF].rearrange("p j (m e) -> p j m e", e=2),
+                    in_=frac[:, :, NF // 2 : NF].unsqueeze(3).to_broadcast([P, JN, NF // 2, 2]),
+                    func=ACT.Sin,
+                    scale=2.0 * math.pi,
+                )
+            else:
+                nc.scalar.activation(
+                    out=sin_t[:, js, HALF:DH].rearrange("p j (m e) -> p j m e", e=2),
+                    in_=frac[:, :, 0 : NF // 2].unsqueeze(3).to_broadcast([P, JN, NF // 2, 2]),
+                    func=ACT.Sin,
+                    scale=-2.0 * math.pi,
+                )
+
+        table_turns(0)
+        table_vector(0)
+
+        wg = const.tile([P, 2, 3 * DH, 4], BF16, align_bytes=64)
+        for wi in range(3):
+            if wi < 2:
+                nc.vector.tensor_copy(
+                    out=wg[:, :, wi * DH : (wi + 1) * DH, :], in_=wraw[:, wi].rearrange("p g t n -> p g n t")
+                )
+            else:
+                nc.gpsimd.tensor_scalar(
+                    out=wg[:, :, wi * DH : (wi + 1) * DH, :],
+                    in0=wraw[:, wi].rearrange("p g t n -> p g n t"),
+                    scalar1=1.0,
+                    scalar2=0.0,
+                    op0=ALU.mult,
+                    op1=ALU.add,
+                )
+        wcod = const.tile([P, 2, 3 * DH], U32, align_bytes=64)
+        wsc = const.tile([P, 2, 3 * DH], U8, align_bytes=64)
+        for c0, c1 in ((0, 2 * DH), (2 * DH, 3 * DH)):
+            for g in range(2):
+                nc.vector.quantize_mx(
+                    out=wcod[:, g, c0:c1].bitcast(FP8X4),
+                    scales=wsc[:, g, c0:c1],
+                    in_=wg[:, g, c0:c1, :].rearrange("p n t -> p (n t)"),
+                )
+
+        def transposes(i):
+            xw = xcs[i // 2][:].bitcast(F32)
+            tiles = []
+            for a in range(2):
+                jj = (i % 2) * 2 + a
+                xt = ps_t.tile([P, 4, P], F32)
+                for u in range(4):
+                    col = jj * (D // 2) + (u // 2) * 2 * P
+                    nc.tensor.transpose(xt[:, u, :], xw[:, col + u % 2 : col + 2 * P : 2], ident[:])
+                tiles.append(xt)
+            xts[i] = tiles
+
+        def regroup_tile(i, a):
+            if a == 0:
+                gr = grp.tile([P, 2 * D], BF16, align_bytes=64)
+                grs[i] = gr
+            grw = grs[i][:].bitcast(F32)
+            nc.scalar.copy(
+                out=grw[:, a * (D // 2) : (a + 1) * (D // 2)].rearrange("p (g r u) -> p g r u", g=2, r=P, u=2),
+                in_=xts[i][a][:].rearrange("p (g u) r -> p g r u", g=2, u=2),
+            )
+
+        def regroup(i):
+            regroup_tile(i, 0)
+            regroup_tile(i, 1)
+
+        def quantise(i):
+            xcod = cod.tile([P, D // 2], U32, align_bytes=64)
+            xsc = cod.tile([P, D // 2], U8, align_bytes=64)
+            nc.vector.quantize_mx(out=xcod[:].bitcast(FP8X4), scales=xsc[:], in_=grs[i][:])
+            cods[i] = (xcod, xsc)
+
+        def multiply(i):
+            xcod, xsc = cods[i]
+            qk = ps_q.tile([P, 4 * DH], F32)
+            vv = ps_v.tile([P, 2 * DH], F32)
+            for a in range(2):
+                for dst, c0, c1 in (
+                    (qk[:, a * 2 * DH : (a + 1) * 2 * DH], 0, 2 * DH),
+                    (vv[:, a * DH : (a + 1) * DH], 2 * DH, 3 * DH),
+                ):
+                    for g in range(2):
+                        cols = slice((a * 2 + g) * P, (a * 2 + g + 1) * P)
+                        nc.tensor.matmul_mx(
+                            out=dst,
+                            lhsT=xcod[:, cols].bitcast(FP8X4),
+                            lhsT_scale=xsc[:, cols],
+                            rhs=wcod[:, g, c0:c1].bitcast(FP8X4),
+                            rhs_scale=wsc[:, g, c0:c1],
+                            start=(g == 0),
+                            stop=(g == 1),
+                        )
+            accs[i] = (qk, vv)
+
+        def store(c, lo, hi):
+            jc, b = chunks[c]
+            js = slice(jc * JN + lo, jc * JN + hi)
+            oqk = oqks[c]
+            for dram, src in (
+                (out_0, oqk[:, 0, lo:hi, :]),
+                (out_1, oqk[:, 1, lo:hi, :]),
+                (out_2, ovs[c][:, lo:hi, :]),
+            ):
+                nc.sync.dma_start(out=dram[b, 0].rearrange("(p j) f -> p j f", j=J)[:, js, :], in_=src)
+
+        def products(i):
+            c = i // 2
+            jc, b = chunks[c]
+            jj0 = (i % 2) * 2
+            j0 = jc * JN + jj0
+            if i % 2 == 0:
+                pt = prod.tile([P, 2, 2, JN, DH], F32)
+                pts[c] = pt
+            for k, table in enumerate((cos_t, sin_t)):
+                nc.vector.tensor_tensor(
+                    out=pts[c][:, k, :, jj0 : jj0 + 2, :].rearrange("p q a f -> p a q f"),
+                    in0=accs[i][0][:].rearrange("p (a q f) -> p a q f", a=2, q=2),
+                    in1=table[:, j0 : j0 + 2, :].unsqueeze(2).to_broadcast([P, 2, 2, DH]),
+                    op=ALU.mult,
+                )
+
+        def vcopy(i):
+            c = i // 2
+            jj0 = (i % 2) * 2
+            if i % 2 == 0:
+                ov = outp.tile([P, JN, DH], F32)
+                ovs[c] = ov
+            nc.scalar.copy(
+                out=ovs[c][:, jj0 : jj0 + 2, :], in_=accs[i][1][:].rearrange("p (a f) -> p a f", a=2)
+            )
+
+        def adds(c, lo, hi, engines):
+            if lo == 0:
+                oqk = outp.tile([P, 2, JN, DH], F32)
+                oqks[c] = oqk
+            for h in range(2):
+                engines[h].tensor_tensor(
+                    out=oqks[c][:, :, lo:hi, h * HALF : (h + 1) * HALF],
+                    in0=pts[c][:, 0, :, lo:hi, h * HALF : (h + 1) * HALF],
+                    in1=pts[c][:, 1, :, lo:hi, (1 - h) * HALF : (2 - h) * HALF],
+                    op=ALU.add,
+                )
+
+        transposes(0)
+        regroup_tile(0, 0)
+        for part in range(5):
+            table_scalar(0, part)
+        regroup_tile(0, 1)
+        transposes(1)
+        regroup(1)
+        for i in range(NP + 1):
+            if i + 2 < NP:
+                transposes(i + 2)
+            if i < NP:
+                quantise(i)
+                multiply(i)
+            if i >= 1:
+                c = (i - 1) // 2
+                products(i - 1)
+                vcopy(i - 1)
+                if c == NCH - 1:
+                    lo = ((i - 1) % 2) * 2
+                    adds(c, lo, lo + 2, (nc.vector if lo > 0 else nc.gpsimd, nc.gpsimd))
+                    store(c, lo, lo + 2)
+                elif (i - 1) % 2 == 1:
+                    adds(c, 0, JN, (nc.gpsimd, nc.vector if c % 2 == 0 else nc.gpsimd))
+                    store(c, 0, JN)
+                    if c + LEAD < NCH:
+                        load(c + LEAD)
+            if i + 2 < NP:
+                regroup(i + 2)
+            nxt = i // 8 + 1
+            if nxt < J // JN:
+                if i % 8 == 0:
+                    table_turns(nxt)
+                elif i % 8 == 1:
+                    table_vector(nxt)
+                elif i % 8 <= 6:
+                    table_scalar(nxt, i % 8 - 2)

@@ -262,8 +262,8 @@ def tile_spikinggroupedslidingattention_pa_t_kernel(tc, x, Wq, Wk, Wv, out_0, ou
             for k, table in enumerate((cos_t, sin_t)):
                 nc.vector.tensor_tensor(
                     out=pts[c][:, k, :, jj0 : jj0 + 2, :].rearrange("p q a f -> p a q f"),
-                    in0=accs[i][0][:].rearrange("p (a q f) -> p a q f", a=2, q=2),
-                    in1=table[:, j0 : j0 + 2, :].unsqueeze(2).to_broadcast([P, 2, 2, DH]),
+                    in0=table[:, j0 : j0 + 2, :].unsqueeze(2).to_broadcast([P, 2, 2, DH]),
+                    in1=accs[i][0][:].rearrange("p (a q f) -> p a q f", a=2, q=2),
                     op=ALU.mult,
                 )
 

@@ -22,6 +22,7 @@ NCH = B * J // JN
 NP = NCH * JN // 2
 LEAD = 8
 NB = 10
+AHEAD = 3
 HALF = DH // 2
 NF = DH // 2
 NSEED = 8
@@ -35,14 +36,14 @@ def tile_spikinggroupedslidingattention_pa_t_kernel(tc, x, Wq, Wk, Wv, out_0, ou
     with ExitStack() as ctx:
         const = ctx.enter_context(tc.tile_pool(name="const", bufs=1))
         xin = ctx.enter_context(tc.tile_pool(name="xin", bufs=NB))
-        grp = ctx.enter_context(tc.tile_pool(name="grp", bufs=4))
+        grp = ctx.enter_context(tc.tile_pool(name="grp", bufs=5))
         cod = ctx.enter_context(tc.tile_pool(name="cod", bufs=3))
         prod = ctx.enter_context(tc.tile_pool(name="prod", bufs=3))
-        outp = ctx.enter_context(tc.tile_pool(name="outp", bufs=4))
-        tb = ctx.enter_context(tc.tile_pool(name="tb", bufs=1))
+        outp = ctx.enter_context(tc.tile_pool(name="outp", bufs=3))
         ps_t = ctx.enter_context(tc.psum_pool(name="ps_t", bufs=4))
-        ps_q = ctx.enter_context(tc.psum_pool(name="ps_q", bufs=2))
-        ps_v = ctx.enter_context(tc.psum_pool(name="ps_v", bufs=2))
+        ps_q = ctx.enter_context(tc.psum_pool(name="ps_q", bufs=3))
+        ps_v = ctx.enter_context(tc.psum_pool(name="ps_v", bufs=1))
+        ctx.enter_context(tc.manual_schedule())
 
         xcs = {}
         xts = {}
@@ -55,39 +56,39 @@ def tile_spikinggroupedslidingattention_pa_t_kernel(tc, x, Wq, Wk, Wv, out_0, ou
 
         def load_part(c, lo, hi):
             jc, b = chunks[c]
+            if lo == 0:
+                xc = xin.tile([P, JN * D], BF16)
+                xcs[c] = xc
             nc.sync.dma_start(
                 out=xcs[c][:, lo * D : hi * D].rearrange("p (j d) -> p j d", j=hi - lo),
                 in_=x[b].rearrange("(p j) d -> p j d", j=J)[:, jc * JN + lo : jc * JN + hi, :],
             )
 
-        def load(c):
-            xc = xin.tile([P, JN * D], BF16)
-            xcs[c] = xc
-            if c > 0:
-                load_part(c, 0, JN)
-
         wraw = const.tile([P, 3, 2, 4, DH], BF16)
-        load(0)
         load_part(0, 0, 1)
-        for wi, w_dram in enumerate((Wq, Wk, Wv)):
+        load_part(0, 1, 2)
+        load_part(0, 2, 4)
+        for wi, w_dram in ((2, Wv), (0, Wq), (1, Wk)):
             nc.sync.dma_start(
                 out=wraw[:, wi].rearrange("p g t n -> p g (t n)"),
                 in_=w_dram.rearrange("(g p t) n -> p g (t n)", g=2, p=P, t=4),
             )
-        load_part(0, 1, 2)
-        load_part(0, 2, JN)
-        for c in range(1, LEAD):
-            load(c)
+        load_part(1, 0, 2)
+        load_part(1, 2, 4)
+        for c in range(2, LEAD):
+            load_part(c, 0, JN)
 
-        ident = const.tile([P, P], F32)
-        make_identity(nc, ident[:])
         pos_i = const.tile([P, J], I32)
         nc.gpsimd.iota(pos_i[:], pattern=[[1, J]], base=0, channel_multiplier=J)
+        ident = const.tile([P, P], F32)
+        make_identity(nc, ident[:])
 
         ones = const.tile([P, NSEED], F32)
         nc.vector.memset(ones[:], 1.0)
         warm = const.tile([P, 1], F32)
         nc.scalar.activation(out=warm[:], in_=ones[:, 0:1], func=ACT.Sin)
+        pos = const.tile([P, J], F32)
+        nc.vector.tensor_copy(out=pos[:], in_=pos_i[:])
         fq = const.tile([P, NF], F32)
         for m in range(NSEED):
             nc.vector.tensor_scalar_mul(
@@ -99,92 +100,71 @@ def tile_spikinggroupedslidingattention_pa_t_kernel(tc, x, Wq, Wk, Wv, out_0, ou
                 out=fq[:, n_have : 2 * n_have], in0=fq[:, 0:n_have], scalar1=THETA ** (-n_have / NF)
             )
             n_have *= 2
-        pos = const.tile([P, J], F32)
-        nc.vector.tensor_copy(out=pos[:], in_=pos_i[:])
 
-        cos_t = const.tile([P, J, DH], F32)
-        sin_t = const.tile([P, J, DH], F32)
-        tabs = {}
-        raws = {}
-        halves = {}
-        squares = {}
+        tab = const.tile([P, J // 2, 2, 2, DH], F32)
+        turns = const.tile([P, J, NF], F32)
+        whole = const.tile([P, J, NF], I32)
+        frac = const.tile([P, J, NF], F32)
+        fabs = const.tile([P, J, NF], F32)
 
-        def table_turns(jc):
-            turns = tb.tile([P, JN, NF], F32)
-            for jj in range(JN):
-                j = jc * JN + jj
-                nc.scalar.activation(out=turns[:, jj, :], in_=fq[:], func=ACT.Copy, scale=pos[:, j : j + 1])
-            whole = tb.tile([P, JN, NF], U32)
-            nc.scalar.copy(out=whole[:], in_=turns[:])
-            raws[jc] = (turns, whole)
+        def table_turns(j0, j1, eng):
+            n = j1 - j0
+            eng.tensor_tensor(
+                out=turns[:, j0:j1, :],
+                in0=fq[:].unsqueeze(1).to_broadcast([P, n, NF]),
+                in1=pos[:, j0:j1].unsqueeze(2).to_broadcast([P, n, NF]),
+                op=ALU.mult,
+            )
 
-        def table_vector(jc):
-            turns, whole = raws[jc]
-            frac = tb.tile([P, JN, NF], F32)
-            nc.vector.tensor_tensor(out=frac[:], in0=turns[:], in1=whole[:].bitcast(I32), op=ALU.subtract)
-            tabs[jc] = frac
+        def table_round(j0, j1):
+            nc.vector.tensor_copy(out=whole[:, j0:j1, :], in_=turns[:, j0:j1, :])
 
-        def table_scalar(jc, part):
-            js = slice(jc * JN, (jc + 1) * JN)
-            frac = tabs[jc]
+        def table_frac(j0, j1):
+            nc.vector.tensor_tensor(
+                out=frac[:, j0:j1, :], in0=turns[:, j0:j1, :], in1=whole[:, j0:j1, :], op=ALU.subtract
+            )
+
+        def table_abs(j0, j1):
+            nc.scalar.activation(out=fabs[:, j0:j1, :], in_=frac[:, j0:j1, :], func=ACT.Abs)
+
+        def table_scalar(j0, j1, part):
+            n = j1 - j0
+            pp = slice(j0 // 2, j1 // 2)
             if part == 0:
-                hs = tb.tile([P, JN, NF], F32)
-                nc.scalar.activation(out=hs[:], in_=frac[:], func=ACT.Sin, scale=math.pi)
-                halves[jc] = hs
-            elif part == 1:
-                sq = tb.tile([P, JN, NF], F32)
-                nc.scalar.activation(out=sq[:], in_=halves[jc][:], func=ACT.Square)
-                squares[jc] = sq
-            elif part == 2:
                 nc.scalar.activation(
-                    out=cos_t[:, js, :].rearrange("p j (m e) -> p j m e", e=2),
-                    in_=squares[jc][:].unsqueeze(3).to_broadcast([P, JN, NF, 2]),
-                    func=ACT.Copy,
-                    bias=1.0,
-                    scale=-2.0,
-                )
-            elif part == 3:
-                nc.scalar.activation(
-                    out=sin_t[:, js, 0:HALF].rearrange("p j (m e) -> p j m e", e=2),
-                    in_=frac[:, :, NF // 2 : NF].unsqueeze(3).to_broadcast([P, JN, NF // 2, 2]),
+                    out=tab[:, pp, 0].rearrange("p c a (m e) -> p c a m e", e=2),
+                    in_=fabs[:, j0:j1, :].rearrange("p (c a) m -> p c a m", a=2).unsqueeze(4).to_broadcast([P, n // 2, 2, NF, 2]),
                     func=ACT.Sin,
-                    scale=2.0 * math.pi,
-                )
-            else:
-                nc.scalar.activation(
-                    out=sin_t[:, js, HALF:DH].rearrange("p j (m e) -> p j m e", e=2),
-                    in_=frac[:, :, 0 : NF // 2].unsqueeze(3).to_broadcast([P, JN, NF // 2, 2]),
-                    func=ACT.Sin,
+                    bias=math.pi / 2.0,
                     scale=-2.0 * math.pi,
                 )
+                return
+            lo, scale = ((HALF, -2.0 * math.pi), (0, 2.0 * math.pi))[part - 1]
+            m0 = (HALF - lo) // 2
+            nc.scalar.activation(
+                out=tab[:, pp, 1, :, lo : lo + HALF].rearrange("p c a (m e) -> p c a m e", e=2),
+                in_=frac[:, j0:j1, m0 : m0 + NF // 2].rearrange("p (c a) m -> p c a m", a=2).unsqueeze(4).to_broadcast([P, n // 2, 2, NF // 2, 2]),
+                func=ACT.Sin,
+                scale=scale,
+            )
 
-        table_turns(0)
-        table_vector(0)
+        wgqk = const.tile([P, 2, 2 * DH, 4], BF16, align_bytes=64)
+        wgv = const.tile([P, 2, DH, 4], BF16, align_bytes=64)
+        cqk = const.tile([P, 2, 2 * DH], U32, align_bytes=64)
+        sqk = const.tile([P, 2, 2 * DH], U8, align_bytes=64)
+        cv = const.tile([P, 2, DH], U32, align_bytes=64)
+        sv = const.tile([P, 2, DH], U8, align_bytes=64)
 
-        wg = const.tile([P, 2, 3 * DH, 4], BF16, align_bytes=64)
-        for wi in range(3):
-            if wi < 2:
-                nc.vector.tensor_copy(
-                    out=wg[:, :, wi * DH : (wi + 1) * DH, :], in_=wraw[:, wi].rearrange("p g t n -> p g n t")
-                )
-            else:
-                nc.gpsimd.tensor_scalar(
-                    out=wg[:, :, wi * DH : (wi + 1) * DH, :],
-                    in0=wraw[:, wi].rearrange("p g t n -> p g n t"),
-                    scalar1=1.0,
-                    scalar2=0.0,
-                    op0=ALU.mult,
-                    op1=ALU.add,
-                )
-        wcod = const.tile([P, 2, 3 * DH], U32, align_bytes=64)
-        wsc = const.tile([P, 2, 3 * DH], U8, align_bytes=64)
-        for c0, c1 in ((0, 2 * DH), (2 * DH, 3 * DH)):
-            for g in range(2):
-                nc.vector.quantize_mx(
-                    out=wcod[:, g, c0:c1].bitcast(FP8X4),
-                    scales=wsc[:, g, c0:c1],
-                    in_=wg[:, g, c0:c1, :].rearrange("p n t -> p (n t)"),
-                )
+        def w_regroup(wi, copy, g0=0, g1=2):
+            dst = wgv[:] if wi == 2 else wgqk[:, :, wi * DH : (wi + 1) * DH, :]
+            copy(out=dst[:, g0:g1], in_=wraw[:, wi, g0:g1].rearrange("p g t n -> p g n t"))
+
+        def w_quantise(codes, scales, grouped):
+            nc.vector.quantize_mx(
+                out=codes[:].rearrange("p g n -> p (g n)").bitcast(FP8X4),
+                scales=scales[:].rearrange("p g n -> p (g n)"),
+                in_=grouped[:].rearrange("p g n t -> p (g n t)"),
+            )
 
         def transposes(i):
             xw = xcs[i // 2][:].bitcast(F32)
@@ -198,34 +178,46 @@ def tile_spikinggroupedslidingattention_pa_t_kernel(tc, x, Wq, Wk, Wv, out_0, ou
                 tiles.append(xt)
             xts[i] = tiles
 
-        def regroup_tile(i, a):
+        def regroup_tile(i, a, copy):
             if a == 0:
                 gr = grp.tile([P, 2 * D], BF16, align_bytes=64)
                 grs[i] = gr
             grw = grs[i][:].bitcast(F32)
-            nc.scalar.copy(
+            copy(
                 out=grw[:, a * (D // 2) : (a + 1) * (D // 2)].rearrange("p (g r u) -> p g r u", g=2, r=P, u=2),
                 in_=xts[i][a][:].rearrange("p (g u) r -> p g r u", g=2, u=2),
             )
 
         def regroup(i):
-            regroup_tile(i, 0)
-            regroup_tile(i, 1)
+            regroup_tile(i, 0, nc.scalar.copy)
+            regroup_tile(i, 1, nc.scalar.copy)
 
-        def quantise(i):
-            xcod = cod.tile([P, D // 2], U32, align_bytes=64)
-            xsc = cod.tile([P, D // 2], U8, align_bytes=64)
-            nc.vector.quantize_mx(out=xcod[:].bitcast(FP8X4), scales=xsc[:], in_=grs[i][:])
-            cods[i] = (xcod, xsc)
-
-        def multiply(i):
+        def quantise(i, lo=0, hi=2):
+            if lo == 0:
+                xcod = cod.tile([P, D // 2], U32, align_bytes=64)
+                xsc = cod.tile([P, D // 2], U8, align_bytes=64)
+                cods[i] = (xcod, xsc)
             xcod, xsc = cods[i]
-            qk = ps_q.tile([P, 4 * DH], F32)
-            vv = ps_v.tile([P, 2 * DH], F32)
-            for a in range(2):
-                for dst, c0, c1 in (
-                    (qk[:, a * 2 * DH : (a + 1) * 2 * DH], 0, 2 * DH),
-                    (vv[:, a * DH : (a + 1) * DH], 2 * DH, 3 * DH),
+            w = slice(lo * (D // 4), hi * (D // 4))
+            nc.vector.quantize_mx(
+                out=xcod[:, w].bitcast(FP8X4), scales=xsc[:, w], in_=grs[i][:, lo * D : hi * D]
+            )
+
+        def multiply(i, lo=0, hi=2):
+            xcod, xsc = cods[i]
+            if lo == 0:
+                qk = ps_q.tile([P, 4 * DH], F32)
+                if i % 2 == 0:
+                    vv = ps_v.tile([P, JN * DH], F32)
+                else:
+                    vv = accs[i - 1][1]
+                accs[i] = (qk, vv)
+            qk, vv = accs[i]
+            for a in range(lo, hi):
+                jj = (i % 2) * 2 + a
+                for dst, codes, scales in (
+                    (qk[:, a * 2 * DH : (a + 1) * 2 * DH], cqk, sqk),
+                    (vv[:, jj * DH : (jj + 1) * DH], cv, sv),
                 ):
                     for g in range(2):
                         cols = slice((a * 2 + g) * P, (a * 2 + g + 1) * P)
@@ -233,95 +225,150 @@ def tile_spikinggroupedslidingattention_pa_t_kernel(tc, x, Wq, Wk, Wv, out_0, ou
                             out=dst,
                             lhsT=xcod[:, cols].bitcast(FP8X4),
                             lhsT_scale=xsc[:, cols],
-                            rhs=wcod[:, g, c0:c1].bitcast(FP8X4),
-                            rhs_scale=wsc[:, g, c0:c1],
+                            rhs=codes[:, g, :].bitcast(FP8X4),
+                            rhs_scale=scales[:, g, :],
                             start=(g == 0),
                             stop=(g == 1),
                         )
-            accs[i] = (qk, vv)
 
         def store(c, lo, hi):
             jc, b = chunks[c]
             js = slice(jc * JN + lo, jc * JN + hi)
             oqk = oqks[c]
             for dram, src in (
+                (out_2, ovs[c][:, lo:hi, :]),
                 (out_0, oqk[:, 0, lo:hi, :]),
                 (out_1, oqk[:, 1, lo:hi, :]),
-                (out_2, ovs[c][:, lo:hi, :]),
             ):
                 nc.sync.dma_start(out=dram[b, 0].rearrange("(p j) f -> p j f", j=J)[:, js, :], in_=src)
+
+        def product_tile(i, a):
+            c = i // 2
+            jc, b = chunks[c]
+            jj = (i % 2) * 2 + a
+            nc.vector.tensor_tensor(
+                out=pts[c][:, :, jj],
+                in0=tab[:, (jc * JN + jj) // 2, :, a].unsqueeze(2).to_broadcast([P, 2, 2, DH]),
+                in1=accs[i][0][:, a * 2 * DH : (a + 1) * 2 * DH].rearrange("p (q f) -> p q f", q=2).unsqueeze(1).to_broadcast([P, 2, 2, DH]),
+                op=ALU.mult,
+            )
 
         def products(i):
             c = i // 2
             jc, b = chunks[c]
             jj0 = (i % 2) * 2
-            j0 = jc * JN + jj0
             if i % 2 == 0:
-                pt = prod.tile([P, 2, 2, JN, DH], F32)
+                pt = prod.tile([P, 2, JN, 2, DH], F32)
                 pts[c] = pt
-            for k, table in enumerate((cos_t, sin_t)):
-                nc.vector.tensor_tensor(
-                    out=pts[c][:, k, :, jj0 : jj0 + 2, :].rearrange("p q a f -> p a q f"),
-                    in0=table[:, j0 : j0 + 2, :].unsqueeze(2).to_broadcast([P, 2, 2, DH]),
-                    in1=accs[i][0][:].rearrange("p (a q f) -> p a q f", a=2, q=2),
-                    op=ALU.mult,
-                )
+            nc.vector.tensor_tensor(
+                out=pts[c][:, :, jj0 : jj0 + 2],
+                in0=tab[:, (jc * JN + jj0) // 2].unsqueeze(3).to_broadcast([P, 2, 2, 2, DH]),
+                in1=accs[i][0][:].rearrange("p (a q f) -> p a q f", a=2, q=2).unsqueeze(1).to_broadcast([P, 2, 2, 2, DH]),
+                op=ALU.mult,
+            )
 
-        def vcopy(i):
-            c = i // 2
-            jj0 = (i % 2) * 2
-            if i % 2 == 0:
+        def vcopy(c, lo, hi):
+            if lo == 0:
                 ov = outp.tile([P, JN, DH], F32)
                 ovs[c] = ov
             nc.scalar.copy(
-                out=ovs[c][:, jj0 : jj0 + 2, :], in_=accs[i][1][:].rearrange("p (a f) -> p a f", a=2)
+                out=ovs[c][:, lo:hi, :], in_=accs[2 * c][1][:, lo * DH : hi * DH].rearrange("p (j f) -> p j f", f=DH)
             )
 
-        def adds(c, lo, hi, engines):
+        def adds(c, lo, hi, engine):
             if lo == 0:
                 oqk = outp.tile([P, 2, JN, DH], F32)
                 oqks[c] = oqk
-            for h in range(2):
-                engines[h].tensor_tensor(
-                    out=oqks[c][:, :, lo:hi, h * HALF : (h + 1) * HALF],
-                    in0=pts[c][:, 0, :, lo:hi, h * HALF : (h + 1) * HALF],
-                    in1=pts[c][:, 1, :, lo:hi, (1 - h) * HALF : (2 - h) * HALF],
-                    op=ALU.add,
-                )
+            engine.tensor_tensor(
+                out=oqks[c][:, :, lo:hi, :].rearrange("p q j (h f) -> p j q h f", h=2),
+                in0=pts[c][:, 0, lo:hi, :, :].rearrange("p j q (h f) -> p j q h f", h=2),
+                in1=pts[c][:, 1, lo:hi, :, :].rearrange("p j q (h f) -> p j q h f", h=2)[:, :, :, ::-1, :],
+                op=ALU.add,
+            )
 
+        V, SC, G = nc.vector.tensor_copy, nc.scalar.copy, nc.gpsimd
+        table_turns(0, JN, nc.vector)
+        table_round(0, JN)
+        table_frac(0, JN)
+        table_abs(0, JN)
+        for part in range(3):
+            table_scalar(0, JN, part)
+        rest = (JN, J)
+        table_turns(*rest, nc.gpsimd)
         transposes(0)
-        regroup_tile(0, 0)
-        for part in range(5):
-            table_scalar(0, part)
-        regroup_tile(0, 1)
+        regroup_tile(0, 0, SC)
+        regroup_tile(0, 1, V)
         transposes(1)
-        regroup(1)
-        for i in range(NP + 1):
-            if i + 2 < NP:
-                transposes(i + 2)
-            if i < NP:
-                quantise(i)
-                multiply(i)
-            if i >= 1:
-                c = (i - 1) // 2
-                products(i - 1)
-                vcopy(i - 1)
-                if c == NCH - 1:
-                    lo = ((i - 1) % 2) * 2
-                    adds(c, lo, lo + 2, (nc.vector if lo > 0 else nc.gpsimd, nc.gpsimd))
-                    store(c, lo, lo + 2)
-                elif (i - 1) % 2 == 1:
-                    adds(c, 0, JN, (nc.gpsimd, nc.vector if c % 2 == 0 else nc.gpsimd))
-                    store(c, 0, JN)
-                    if c + LEAD < NCH:
-                        load(c + LEAD)
-            if i + 2 < NP:
-                regroup(i + 2)
+        w_regroup(2, SC)
+        w_regroup(0, V)
+        regroup_tile(1, 0, V)
+        regroup_tile(1, 1, SC)
+        w_regroup(1, V, 0, 1)
+        w_regroup(1, SC, 1, 2)
+        quantise(0)
+        w_quantise(cqk, sqk, wgqk)
+        w_quantise(cv, sv, wgv)
+        transposes(2)
+        regroup(2)
+        multiply(0)
+        quantise(1)
+        transposes(3)
+        regroup(3)
+        def finish(i):
+            c = i // 2
+            lo = (i % 2) * 2
+            adds(c, lo, lo + 2, G)
+            if lo > 0:
+                store(c, 0, JN)
+                if c + LEAD < NCH:
+                    load_part(c + LEAD, 0, JN)
+
+        LAST = NP - 1
+        for i in range(1, LAST - 3):
+            multiply(i)
+            if i % 2 == 1:
+                vcopy(i // 2, 0, JN)
+            transposes(i + AHEAD)
+            regroup(i + AHEAD)
+            products(i - 1)
+            quantise(i + 1)
+            finish(i - 1)
+            if i == 1:
+                table_round(*rest)
+            elif i == 2:
+                table_frac(*rest)
             nxt = i // 8 + 1
             if nxt < J // JN:
-                if i % 8 == 0:
-                    table_turns(nxt)
-                elif i % 8 == 1:
-                    table_vector(nxt)
-                elif i % 8 <= 6:
-                    table_scalar(nxt, i % 8 - 2)
+                k = i % 8
+                if k == 3 and nxt == 1:
+                    table_abs(*rest)
+                elif 4 <= k <= 6:
+                    table_scalar(nxt * JN, (nxt + 1) * JN, k - 4)
+        multiply(LAST - 3)
+        products(LAST - 4)
+        quantise(LAST - 2)
+        finish(LAST - 4)
+        multiply(LAST - 2)
+        vcopy((LAST - 2) // 2, 0, JN)
+        transposes(LAST)
+        regroup_tile(LAST, 0, SC)
+        regroup_tile(LAST, 1, SC)
+        products(LAST - 3)
+        quantise(LAST - 1)
+        finish(LAST - 3)
+        multiply(LAST - 1)
+        products(LAST - 2)
+        quantise(LAST, 0, 1)
+        quantise(LAST, 1, 2)
+        finish(LAST - 2)
+        multiply(LAST, 0, 1)
+        multiply(LAST, 1, 2)
+        products(LAST - 1)
+        c = NCH - 1
+        vcopy(c, 0, 4)
+        product_tile(LAST, 0)
+        product_tile(LAST, 1)
+        adds(c, 0, 2, nc.vector)
+        store(c, 0, 2)
+        adds(c, 2, 4, nc.vector)
+        store(c, 2, 4)

@@ -38,6 +38,7 @@ def tile_spikinggroupedslidingattention_pa_t_kernel(tc, x, Wq, Wk, Wv, out_0, ou
         xin = ctx.enter_context(tc.tile_pool(name="xin", bufs=NB))
         grp = ctx.enter_context(tc.tile_pool(name="grp", bufs=5))
         cod = ctx.enter_context(tc.tile_pool(name="cod", bufs=3))
+        srt = ctx.enter_context(tc.tile_pool(name="srt", bufs=4))
         prod = ctx.enter_context(tc.tile_pool(name="prod", bufs=3))
         outp = ctx.enter_context(tc.tile_pool(name="outp", bufs=3))
         ps_t = ctx.enter_context(tc.psum_pool(name="ps_t", bufs=4))
@@ -53,6 +54,7 @@ def tile_spikinggroupedslidingattention_pa_t_kernel(tc, x, Wq, Wk, Wv, out_0, ou
         oqks = {}
         pts = {}
         ovs = {}
+        sorts = {}
 
         def load_part(c, lo, hi):
             jc, b = chunks[c]
@@ -166,6 +168,16 @@ def tile_spikinggroupedslidingattention_pa_t_kernel(tc, x, Wq, Wk, Wv, out_0, ou
                 in_=grouped[:].rearrange("p g n t -> p (g n t)"),
             )
 
+        def sort_words(i, a):
+            xw = xcs[i // 2][:].bitcast(F32)
+            jj = (i % 2) * 2 + a
+            sw = srt.tile([P, 4, P], F32)
+            sorts[i, a] = sw
+            nc.scalar.copy(
+                out=sw[:].rearrange("p (g u) w -> p g u w", g=2),
+                in_=xw[:, jj * (D // 2) : (jj + 1) * (D // 2)].rearrange("p (g w u) -> p g u w", g=2, u=2),
+            )
+
         def transposes(i):
             xw = xcs[i // 2][:].bitcast(F32)
             tiles = []
@@ -173,8 +185,12 @@ def tile_spikinggroupedslidingattention_pa_t_kernel(tc, x, Wq, Wk, Wv, out_0, ou
                 jj = (i % 2) * 2 + a
                 xt = ps_t.tile([P, 4, P], F32)
                 for u in range(4):
-                    col = jj * (D // 2) + (u // 2) * 2 * P
-                    nc.tensor.transpose(xt[:, u, :], xw[:, col + u % 2 : col + 2 * P : 2], ident[:])
+                    if (i, a) in sorts:
+                        words = sorts[i, a][:, u, :]
+                    else:
+                        col = jj * (D // 2) + (u // 2) * 2 * P
+                        words = xw[:, col + u % 2 : col + 2 * P : 2]
+                    nc.tensor.transpose(xt[:, u, :], words, ident[:])
                 tiles.append(xt)
             xts[i] = tiles
 
@@ -328,6 +344,8 @@ def tile_spikinggroupedslidingattention_pa_t_kernel(tc, x, Wq, Wk, Wv, out_0, ou
             multiply(i)
             if i % 2 == 1:
                 vcopy(i // 2, 0, JN)
+            if i + 5 < NP and i >= 5 and i % 2 == 0:
+                sort_words(i + 5, 0)
             transposes(i + AHEAD)
             regroup(i + AHEAD)
             products(i - 1)

@@ -40,10 +40,10 @@ def tile_spikinggroupedslidingattention_pa_t_kernel(tc, x, Wq, Wk, Wv, out_0, ou
         cod = ctx.enter_context(tc.tile_pool(name="cod", bufs=3))
         srt = ctx.enter_context(tc.tile_pool(name="srt", bufs=4))
         prod = ctx.enter_context(tc.tile_pool(name="prod", bufs=3))
-        outp = ctx.enter_context(tc.tile_pool(name="outp", bufs=3))
+        outp = ctx.enter_context(tc.tile_pool(name="outp", bufs=4))
         ps_t = ctx.enter_context(tc.psum_pool(name="ps_t", bufs=4))
-        ps_q = ctx.enter_context(tc.psum_pool(name="ps_q", bufs=3))
-        ps_v = ctx.enter_context(tc.psum_pool(name="ps_v", bufs=1))
+        ps_q = ctx.enter_context(tc.psum_pool(name="ps_q", bufs=2))
+        ps_v = ctx.enter_context(tc.psum_pool(name="ps_v", bufs=2))
         ctx.enter_context(tc.manual_schedule())
 
         xcs = {}
@@ -67,14 +67,15 @@ def tile_spikinggroupedslidingattention_pa_t_kernel(tc, x, Wq, Wk, Wv, out_0, ou
             )
 
         wraw = const.tile([P, 3, 2, 4, DH], BF16)
-        load_part(0, 0, 1)
-        load_part(0, 1, 2)
-        load_part(0, 2, 4)
         for wi, w_dram in ((2, Wv), (0, Wq), (1, Wk)):
             nc.sync.dma_start(
                 out=wraw[:, wi].rearrange("p g t n -> p g (t n)"),
                 in_=w_dram.rearrange("(g p t) n -> p g (t n)", g=2, p=P, t=4),
             )
+        load_part(0, 0, 1)
+        load_part(0, 1, 2)
+        load_part(0, 2, 3)
+        load_part(0, 3, 4)
         load_part(1, 0, 2)
         load_part(1, 2, 4)
         for c in range(2, LEAD):
@@ -307,23 +308,22 @@ def tile_spikinggroupedslidingattention_pa_t_kernel(tc, x, Wq, Wk, Wv, out_0, ou
         table_round(0, JN)
         table_frac(0, JN)
         table_abs(0, JN)
-        for part in range(3):
-            table_scalar(0, JN, part)
         rest = (JN, J)
-        table_turns(*rest, nc.gpsimd)
-        transposes(0)
-        regroup_tile(0, 0, SC)
-        regroup_tile(0, 1, V)
-        transposes(1)
+        table_turns(*rest, nc.vector)
         w_regroup(2, SC)
         w_regroup(0, V)
-        regroup_tile(1, 0, V)
-        regroup_tile(1, 1, SC)
-        w_regroup(1, V, 0, 1)
-        w_regroup(1, SC, 1, 2)
-        quantise(0)
+        w_regroup(1, V)
+        table_scalar(0, JN, 0)
+        table_scalar(0, JN, 1)
         w_quantise(cqk, sqk, wgqk)
+        transposes(0)
+        regroup_tile(0, 0, V)
+        regroup_tile(0, 1, SC)
         w_quantise(cv, sv, wgv)
+        quantise(0)
+        transposes(1)
+        table_scalar(0, JN, 2)
+        regroup(1)
         transposes(2)
         regroup(2)
         multiply(0)
@@ -344,7 +344,7 @@ def tile_spikinggroupedslidingattention_pa_t_kernel(tc, x, Wq, Wk, Wv, out_0, ou
             multiply(i)
             if i % 2 == 1:
                 vcopy(i // 2, 0, JN)
-            if i + 5 < NP and i >= 5 and i % 2 == 0:
+            if i + 5 < NP and i >= 5 and i % 2 == 0 and not (i < 24 and i % 8 == 4):
                 sort_words(i + 5, 0)
             transposes(i + AHEAD)
             regroup(i + AHEAD)
@@ -384,9 +384,10 @@ def tile_spikinggroupedslidingattention_pa_t_kernel(tc, x, Wq, Wk, Wv, out_0, ou
         products(LAST - 1)
         c = NCH - 1
         vcopy(c, 0, 4)
+        adds(c, 0, 1, G)
         product_tile(LAST, 0)
         product_tile(LAST, 1)
-        adds(c, 0, 2, nc.vector)
+        adds(c, 1, 2, nc.vector)
         store(c, 0, 2)
         adds(c, 2, 4, nc.vector)
         store(c, 2, 4)

@@ -153,10 +153,10 @@ def tile_spikinggroupedslidingattention_pa_t_kernel(tc, x, Wq, Wk, Wv, out_0, ou
 
         wgqk = const.tile([P, 2, 2 * DH, 4], BF16, align_bytes=64)
         wgv = const.tile([P, 2, DH, 4], BF16, align_bytes=64)
-        cqk = const.tile([P, 2, 2 * DH], U32, align_bytes=64)
-        sqk = const.tile([P, 2, 2 * DH], U8, align_bytes=64)
-        cv = const.tile([P, 2, DH], U32, align_bytes=64)
-        sv = const.tile([P, 2, DH], U8, align_bytes=64)
+        cqk = const.tile([P, 2, 2 * DH], U32, align_bytes=256)
+        sqk = const.tile([P, 2, 2 * DH], U8, align_bytes=256)
+        cv = const.tile([P, 2, DH], U32, align_bytes=256)
+        sv = const.tile([P, 2, DH], U8, align_bytes=256)
 
         def w_regroup(wi, copy, g0=0, g1=2):
             dst = wgv[:] if wi == 2 else wgqk[:, :, wi * DH : (wi + 1) * DH, :]
@@ -211,8 +211,8 @@ def tile_spikinggroupedslidingattention_pa_t_kernel(tc, x, Wq, Wk, Wv, out_0, ou
 
         def quantise(i, lo=0, hi=2):
             if lo == 0:
-                xcod = cod.tile([P, D // 2], U32, align_bytes=64)
-                xsc = cod.tile([P, D // 2], U8, align_bytes=64)
+                xcod = cod.tile([P, D // 2], U32, align_bytes=256)
+                xsc = cod.tile([P, D // 2], U8, align_bytes=256)
                 cods[i] = (xcod, xsc)
             xcod, xsc = cods[i]
             w = slice(lo * (D // 4), hi * (D // 4))
@@ -248,16 +248,21 @@ def tile_spikinggroupedslidingattention_pa_t_kernel(tc, x, Wq, Wk, Wv, out_0, ou
                             stop=(g == 1),
                         )
 
-        def store(c, lo, hi):
+        def store_rows(dram, c, lo, hi, src):
             jc, b = chunks[c]
             js = slice(jc * JN + lo, jc * JN + hi)
-            oqk = oqks[c]
-            for dram, src in (
-                (out_2, ovs[c][:, lo:hi, :]),
-                (out_0, oqk[:, 0, lo:hi, :]),
-                (out_1, oqk[:, 1, lo:hi, :]),
-            ):
-                nc.sync.dma_start(out=dram[b, 0].rearrange("(p j) f -> p j f", j=J)[:, js, :], in_=src)
+            nc.sync.dma_start(out=dram[b, 0].rearrange("(p j) f -> p j f", j=J)[:, js, :], in_=src)
+
+        def store_v(c):
+            store_rows(out_2, c, 0, JN, ovs[c][:])
+
+        def store_qk(c, lo, hi):
+            store_rows(out_0, c, lo, hi, oqks[c][:, 0, lo:hi, :])
+            store_rows(out_1, c, lo, hi, oqks[c][:, 1, lo:hi, :])
+
+        def store(c):
+            store_v(c)
+            store_qk(c, 0, JN)
 
         def product_tile(i, a):
             c = i // 2
@@ -321,6 +326,7 @@ def tile_spikinggroupedslidingattention_pa_t_kernel(tc, x, Wq, Wk, Wv, out_0, ou
         regroup_tile(0, 1, SC)
         w_quantise(cv, sv, wgv)
         quantise(0)
+        table_round(*rest)
         transposes(1)
         table_scalar(0, JN, 2)
         regroup(1)
@@ -328,6 +334,8 @@ def tile_spikinggroupedslidingattention_pa_t_kernel(tc, x, Wq, Wk, Wv, out_0, ou
         regroup(2)
         multiply(0)
         quantise(1)
+        table_frac(*rest)
+        table_abs(*rest)
         transposes(3)
         regroup(3)
         def finish(i):
@@ -335,7 +343,7 @@ def tile_spikinggroupedslidingattention_pa_t_kernel(tc, x, Wq, Wk, Wv, out_0, ou
             lo = (i % 2) * 2
             adds(c, lo, lo + 2, G)
             if lo > 0:
-                store(c, 0, JN)
+                store(c)
                 if c + LEAD < NCH:
                     load_part(c + LEAD, 0, JN)
 
@@ -351,17 +359,9 @@ def tile_spikinggroupedslidingattention_pa_t_kernel(tc, x, Wq, Wk, Wv, out_0, ou
             products(i - 1)
             quantise(i + 1)
             finish(i - 1)
-            if i == 1:
-                table_round(*rest)
-            elif i == 2:
-                table_frac(*rest)
-            nxt = i // 8 + 1
-            if nxt < J // JN:
-                k = i % 8
-                if k == 3 and nxt == 1:
-                    table_abs(*rest)
-                elif 4 <= k <= 6:
-                    table_scalar(nxt * JN, (nxt + 1) * JN, k - 4)
+            jc, part = divmod(i, 8) if i < 24 else (3, 0)
+            if jc + 1 < J // JN and 1 <= part <= 3:
+                table_scalar((jc + 1) * JN, (jc + 2) * JN, part - 1)
         multiply(LAST - 3)
         products(LAST - 4)
         quantise(LAST - 2)
@@ -384,10 +384,11 @@ def tile_spikinggroupedslidingattention_pa_t_kernel(tc, x, Wq, Wk, Wv, out_0, ou
         products(LAST - 1)
         c = NCH - 1
         vcopy(c, 0, 4)
+        store_v(c)
         adds(c, 0, 1, G)
         product_tile(LAST, 0)
         product_tile(LAST, 1)
         adds(c, 1, 2, nc.vector)
-        store(c, 0, 2)
+        store_qk(c, 0, 2)
         adds(c, 2, 4, nc.vector)
-        store(c, 2, 4)
+        store_qk(c, 2, 4)

@@ -76,7 +76,8 @@ def tile_spikinggroupedslidingattention_pa_t_kernel(tc, x, Wq, Wk, Wv, out_0, ou
         load_part(0, 1, 2)
         load_part(0, 2, 3)
         load_part(0, 3, 4)
-        load_part(1, 0, 2)
+        load_part(1, 0, 1)
+        load_part(1, 1, 2)
         load_part(1, 2, 4)
         for c in range(2, LEAD):
             load_part(c, 0, JN)
@@ -230,12 +231,13 @@ def tile_spikinggroupedslidingattention_pa_t_kernel(tc, x, Wq, Wk, Wv, out_0, ou
                     vv = accs[i - 1][1]
                 accs[i] = (qk, vv)
             qk, vv = accs[i]
-            for a in range(lo, hi):
-                jj = (i % 2) * 2 + a
-                for dst, codes, scales in (
-                    (qk[:, a * 2 * DH : (a + 1) * 2 * DH], cqk, sqk),
-                    (vv[:, jj * DH : (jj + 1) * DH], cv, sv),
-                ):
+            for part in range(2):
+                for a in range(lo, hi):
+                    jj = (i % 2) * 2 + a
+                    dst, codes, scales = (
+                        (qk[:, a * 2 * DH : (a + 1) * 2 * DH], cqk, sqk),
+                        (vv[:, jj * DH : (jj + 1) * DH], cv, sv),
+                    )[part]
                     for g in range(2):
                         cols = slice((a * 2 + g) * P, (a * 2 + g + 1) * P)
                         nc.tensor.matmul_mx(
@@ -253,15 +255,15 @@ def tile_spikinggroupedslidingattention_pa_t_kernel(tc, x, Wq, Wk, Wv, out_0, ou
             js = slice(jc * JN + lo, jc * JN + hi)
             nc.sync.dma_start(out=dram[b, 0].rearrange("(p j) f -> p j f", j=J)[:, js, :], in_=src)
 
-        def store_v(c):
-            store_rows(out_2, c, 0, JN, ovs[c][:])
+        def store_v(c, lo, hi):
+            store_rows(out_2, c, lo, hi, ovs[c][:, lo:hi, :])
 
         def store_qk(c, lo, hi):
             store_rows(out_0, c, lo, hi, oqks[c][:, 0, lo:hi, :])
             store_rows(out_1, c, lo, hi, oqks[c][:, 1, lo:hi, :])
 
         def store(c):
-            store_v(c)
+            store_v(c, 0, JN)
             store_qk(c, 0, JN)
 
         def product_tile(i, a):
@@ -366,28 +368,31 @@ def tile_spikinggroupedslidingattention_pa_t_kernel(tc, x, Wq, Wk, Wv, out_0, ou
         products(LAST - 4)
         quantise(LAST - 2)
         finish(LAST - 4)
-        multiply(LAST - 2)
-        vcopy((LAST - 2) // 2, 0, JN)
         transposes(LAST)
         regroup_tile(LAST, 0, SC)
         regroup_tile(LAST, 1, SC)
+        multiply(LAST - 2)
+        c = NCH - 2
+        vcopy(c, 0, JN)
+        store_v(c, 0, JN)
         products(LAST - 3)
         quantise(LAST - 1)
-        finish(LAST - 3)
+        adds(c, 0, 2, G)
+        store_qk(c, 0, 2)
         multiply(LAST - 1)
+        vcopy(c + 1, 0, 2)
+        store_v(c + 1, 0, 2)
         products(LAST - 2)
-        quantise(LAST, 0, 1)
-        quantise(LAST, 1, 2)
-        finish(LAST - 2)
-        multiply(LAST, 0, 1)
-        multiply(LAST, 1, 2)
+        quantise(LAST)
+        adds(c, 2, 4, G)
+        store_qk(c, 2, 4)
+        multiply(LAST)
         products(LAST - 1)
         c = NCH - 1
-        vcopy(c, 0, 4)
-        store_v(c)
+        vcopy(c, 2, 4)
+        store_v(c, 2, 4)
         adds(c, 0, 1, G)
-        product_tile(LAST, 0)
-        product_tile(LAST, 1)
+        products(LAST)
         adds(c, 1, 2, nc.vector)
         store_qk(c, 0, 2)
         adds(c, 2, 4, nc.vector)

@@ -354,7 +354,7 @@ def tile_spikinggroupedslidingattention_pa_t_kernel(tc, x, Wq, Wk, Wv, out_0, ou
             multiply(i)
             if i % 2 == 1:
                 vcopy(i // 2, 0, JN)
-            if i + 5 < NP and i >= 5 and i % 2 == 0 and not (i < 24 and i % 8 == 4):
+            if i + 5 < NP and i >= 5 and i % 2 == 0 and not (i < 24 and i % 8 == 2):
                 sort_words(i + 5, 0)
             transposes(i + AHEAD)
             regroup(i + AHEAD)

import math
from contextlib import ExitStack

import concourse.mybir as mybir
from concourse.masks import make_identity

F32 = mybir.dt.float32
BF16 = mybir.dt.bfloat16
I32 = mybir.dt.int32
U32 = mybir.dt.uint32
U8 = mybir.dt.uint8
FP8X4 = mybir.dt.float8_e4m3fn_x4
ALU = mybir.AluOpType
ACT = mybir.ActivationFunctionType

B, S, D, DH = 4, 2048, 1024, 128
THETA = 10000.0
P = 128
J = S // P
JN = 4
NCH = B * J // JN
NP = NCH * JN // 2
LEAD = 8
NB = 10
AHEAD = 3
HALF = DH // 2
NF = DH // 2
NSEED = 8

FLOPS = 2 * B * S * D * 3 * DH


def tile_spikinggroupedslidingattention_pa_t_kernel(tc, x, Wq, Wk, Wv, out_0, out_1, out_2):
    nc = tc.nc
    chunks = [(jc, b) for jc in range(J // JN) for b in range(B)]
    with ExitStack() as ctx:
        const = ctx.enter_context(tc.tile_pool(name="const", bufs=1))
        xin = ctx.enter_context(tc.tile_pool(name="xin", bufs=NB))
        grp = ctx.enter_context(tc.tile_pool(name="grp", bufs=5))
        cod = ctx.enter_context(tc.tile_pool(name="cod", bufs=3))
        srt = ctx.enter_context(tc.tile_pool(name="srt", bufs=4))
        prod = ctx.enter_context(tc.tile_pool(name="prod", bufs=3))
        outp = ctx.enter_context(tc.tile_pool(name="outp", bufs=4))
        ps_t = ctx.enter_context(tc.psum_pool(name="ps_t", bufs=4))
        ps_q = ctx.enter_context(tc.psum_pool(name="ps_q", bufs=2))
        ps_v = ctx.enter_context(tc.psum_pool(name="ps_v", bufs=2))
        ctx.enter_context(tc.manual_schedule())

        xcs = {}
        xts = {}
        grs = {}
        cods = {}
        accs = {}
        oqks = {}
        pts = {}
        ovs = {}
        sorts = {}

        def load_part(c, lo, hi):
            jc, b = chunks[c]
            if lo == 0:
                xc = xin.tile([P, JN * D], BF16)
                xcs[c] = xc
            nc.sync.dma_start(
                out=xcs[c][:, lo * D : hi * D].rearrange("p (j d) -> p j d", j=hi - lo),
                in_=x[b].rearrange("(p j) d -> p j d", j=J)[:, jc * JN + lo : jc * JN + hi, :],
            )

        wraw = const.tile([P, 3, 2, 4, DH], BF16)
        for wi, w_dram in ((2, Wv), (0, Wq), (1, Wk)):
            nc.sync.dma_start(
                out=wraw[:, wi].rearrange("p g t n -> p g (t n)"),
                in_=w_dram.rearrange("(g p t) n -> p g (t n)", g=2, p=P, t=4),
            )
        load_part(0, 0, 1)
        load_part(0, 1, 2)
        load_part(0, 2, 3)
        load_part(0, 3, 4)
        load_part(1, 0, 1)
        load_part(1, 1, 2)
        load_part(1, 2, 4)
        for c in range(2, LEAD):
            load_part(c, 0, JN)

        pos_i = const.tile([P, J], I32)
        nc.gpsimd.iota(pos_i[:], pattern=[[1, J]], base=0, channel_multiplier=J)
        ident = const.tile([P, P], F32)
        make_identity(nc, ident[:])

        ones = const.tile([P, NSEED], F32)
        nc.vector.memset(ones[:], 1.0)
        warm = const.tile([P, 1], F32)
        nc.scalar.activation(out=warm[:], in_=ones[:, 0:1], func=ACT.Sin)
        pos = const.tile([P, J], F32)
        nc.vector.tensor_copy(out=pos[:], in_=pos_i[:])
        fq = const.tile([P, NF], F32)
        for m in range(NSEED):
            nc.vector.tensor_scalar_mul(
                out=fq[:, m : m + 1], in0=ones[:, m : m + 1], scalar1=THETA ** (-m / NF) / (2.0 * math.pi)
            )
        n_have = NSEED
        while n_have < NF:
            nc.vector.tensor_scalar_mul(
                out=fq[:, n_have : 2 * n_have], in0=fq[:, 0:n_have], scalar1=THETA ** (-n_have / NF)
            )
            n_have *= 2

        tab = const.tile([P, J // 2, 2, 2, DH], F32)
        turns = const.tile([P, J, NF], F32)
        whole = const.tile([P, J, NF], I32)
        frac = const.tile([P, J, NF], F32)
        fabs = const.tile([P, J, NF], F32)

        def table_turns(j0, j1, eng):
            n = j1 - j0
            eng.tensor_tensor(
                out=turns[:, j0:j1, :],
                in0=fq[:].unsqueeze(1).to_broadcast([P, n, NF]),
                in1=pos[:, j0:j1].unsqueeze(2).to_broadcast([P, n, NF]),
                op=ALU.mult,
            )

        def table_round(j0, j1):
            nc.vector.tensor_copy(out=whole[:, j0:j1, :], in_=turns[:, j0:j1, :])

        def table_frac(j0, j1):
            nc.vector.tensor_tensor(
                out=frac[:, j0:j1, :], in0=turns[:, j0:j1, :], in1=whole[:, j0:j1, :], op=ALU.subtract
            )

        def table_abs(j0, j1):
            nc.scalar.activation(out=fabs[:, j0:j1, :], in_=frac[:, j0:j1, :], func=ACT.Abs)

        def table_scalar(j0, j1, part):
            n = j1 - j0
            pp = slice(j0 // 2, j1 // 2)
            if part == 0:
                nc.scalar.activation(
                    out=tab[:, pp, 0].rearrange("p c a (m e) -> p c a m e", e=2),
                    in_=fabs[:, j0:j1, :].rearrange("p (c a) m -> p c a m", a=2).unsqueeze(4).to_broadcast([P, n // 2, 2, NF, 2]),
                    func=ACT.Sin,
                    bias=math.pi / 2.0,
                    scale=-2.0 * math.pi,
                )
                return
            lo, scale = ((HALF, -2.0 * math.pi), (0, 2.0 * math.pi))[part - 1]
            m0 = (HALF - lo) // 2
            nc.scalar.activation(
                out=tab[:, pp, 1, :, lo : lo + HALF].rearrange("p c a (m e) -> p c a m e", e=2),
                in_=frac[:, j0:j1, m0 : m0 + NF // 2].rearrange("p (c a) m -> p c a m", a=2).unsqueeze(4).to_broadcast([P, n // 2, 2, NF // 2, 2]),
                func=ACT.Sin,
                scale=scale,
            )

        wgqk = const.tile([P, 2, 2 * DH, 4], BF16, align_bytes=64)
        wgv = const.tile([P, 2, DH, 4], BF16, align_bytes=64)
        cqk = const.tile([P, 2, 2 * DH], U32, align_bytes=256)
        sqk = const.tile([P, 2, 2 * DH], U8, align_bytes=256)
        cv = const.tile([P, 2, DH], U32, align_bytes=256)
        sv = const.tile([P, 2, DH], U8, align_bytes=256)

        def w_regroup(wi, copy, g0=0, g1=2):
            dst = wgv[:] if wi == 2 else wgqk[:, :, wi * DH : (wi + 1) * DH, :]
            copy(out=dst[:, g0:g1], in_=wraw[:, wi, g0:g1].rearrange("p g t n -> p g n t"))

        def w_quantise(codes, scales, grouped):
            nc.vector.quantize_mx(
                out=codes[:].rearrange("p g n -> p (g n)").bitcast(FP8X4),
                scales=scales[:].rearrange("p g n -> p (g n)"),
                in_=grouped[:].rearrange("p g n t -> p (g n t)"),
            )

        def sort_words(i, a):
            xw = xcs[i // 2][:].bitcast(F32)
            jj = (i % 2) * 2 + a
            sw = srt.tile([P, 4, P], F32)
            sorts[i, a] = sw
            nc.scalar.copy(
                out=sw[:].rearrange("p (g u) w -> p g u w", g=2),
                in_=xw[:, jj * (D // 2) : (jj + 1) * (D // 2)].rearrange("p (g w u) -> p g u w", g=2, u=2),
            )

        def transposes(i):
            xw = xcs[i // 2][:].bitcast(F32)
            tiles = []
            for a in range(2):
                jj = (i % 2) * 2 + a
                xt = ps_t.tile([P, 4, P], F32)
                for u in range(4):
                    if (i, a) in sorts:
                        words = sorts[i, a][:, u, :]
                    else:
                        col = jj * (D // 2) + (u // 2) * 2 * P
                        words = xw[:, col + u % 2 : col + 2 * P : 2]
                    nc.tensor.transpose(xt[:, u, :], words, ident[:])
                tiles.append(xt)
            xts[i] = tiles

        def regroup_tile(i, a, copy):
            if a == 0:
                gr = grp.tile([P, 2 * D], BF16, align_bytes=64)
                grs[i] = gr
            grw = grs[i][:].bitcast(F32)
            copy(
                out=grw[:, a * (D // 2) : (a + 1) * (D // 2)].rearrange("p (g r u) -> p g r u", g=2, r=P, u=2),
                in_=xts[i][a][:].rearrange("p (g u) r -> p g r u", g=2, u=2),
            )

        def regroup(i):
            regroup_tile(i, 0, nc.scalar.copy)
            regroup_tile(i, 1, nc.scalar.copy)

        def quantise(i, lo=0, hi=2):
            if lo == 0:
                xcod = cod.tile([P, D // 2], U32, align_bytes=256)
                xsc = cod.tile([P, D // 2], U8, align_bytes=256)
                cods[i] = (xcod, xsc)
            xcod, xsc = cods[i]
            w = slice(lo * (D // 4), hi * (D // 4))
            nc.vector.quantize_mx(
                out=xcod[:, w].bitcast(FP8X4), scales=xsc[:, w], in_=grs[i][:, lo * D : hi * D]
            )

        def multiply(i, lo=0, hi=2):
            xcod, xsc = cods[i]
            if lo == 0:
                qk = ps_q.tile([P, 4 * DH], F32)
                if i % 2 == 0:
                    vv = ps_v.tile([P, JN * DH], F32)
                else:
                    vv = accs[i - 1][1]
                accs[i] = (qk, vv)
            qk, vv = accs[i]
            for part in range(2):
                for a in range(lo, hi):
                    jj = (i % 2) * 2 + a
                    dst, codes, scales = (
                        (qk[:, a * 2 * DH : (a + 1) * 2 * DH], cqk, sqk),
                        (vv[:, jj * DH : (jj + 1) * DH], cv, sv),
                    )[part]
                    for g in range(2):
                        cols = slice((a * 2 + g) * P, (a * 2 + g + 1) * P)
                        nc.tensor.matmul_mx(
                            out=dst,
                            lhsT=xcod[:, cols].bitcast(FP8X4),
                            lhsT_scale=xsc[:, cols],
                            rhs=codes[:, g, :].bitcast(FP8X4),
                            rhs_scale=scales[:, g, :],
                            start=(g == 0),
                            stop=(g == 1),
                        )

        def store_rows(dram, c, lo, hi, src):
            jc, b = chunks[c]
            js = slice(jc * JN + lo, jc * JN + hi)
            nc.sync.dma_start(out=dram[b, 0].rearrange("(p j) f -> p j f", j=J)[:, js, :], in_=src)

        def store_v(c, lo, hi):
            store_rows(out_2, c, lo, hi, ovs[c][:, lo:hi, :])

        def store_qk(c, lo, hi):
            store_rows(out_0, c, lo, hi, oqks[c][:, 0, lo:hi, :])
            store_rows(out_1, c, lo, hi, oqks[c][:, 1, lo:hi, :])

        def store(c):
            store_v(c, 0, JN)
            store_qk(c, 0, JN)

        def product_tile(i, a):
            c = i // 2
            jc, b = chunks[c]
            jj = (i % 2) * 2 + a
            nc.vector.tensor_tensor(
                out=pts[c][:, :, jj],
                in0=tab[:, (jc * JN + jj) // 2, :, a].unsqueeze(2).to_broadcast([P, 2, 2, DH]),
                in1=accs[i][0][:, a * 2 * DH : (a + 1) * 2 * DH].rearrange("p (q f) -> p q f", q=2).unsqueeze(1).to_broadcast([P, 2, 2, DH]),
                op=ALU.mult,
            )

        def products(i):
            c = i // 2
            jc, b = chunks[c]
            jj0 = (i % 2) * 2
            if i % 2 == 0:
                pt = prod.tile([P, 2, JN, 2, DH], F32)
                pts[c] = pt
            nc.vector.tensor_tensor(
                out=pts[c][:, :, jj0 : jj0 + 2],
                in0=tab[:, (jc * JN + jj0) // 2].unsqueeze(3).to_broadcast([P, 2, 2, 2, DH]),
                in1=accs[i][0][:].rearrange("p (a q f) -> p a q f", a=2, q=2).unsqueeze(1).to_broadcast([P, 2, 2, 2, DH]),
                op=ALU.mult,
            )

        def vcopy(c, lo, hi):
            if lo == 0:
                ov = outp.tile([P, JN, DH], F32)
                ovs[c] = ov
            nc.scalar.copy(
                out=ovs[c][:, lo:hi, :], in_=accs[2 * c][1][:, lo * DH : hi * DH].rearrange("p (j f) -> p j f", f=DH)
            )

        def adds(c, lo, hi, engine):
            if lo == 0:
                oqk = outp.tile([P, 2, JN, DH], F32)
                oqks[c] = oqk
            engine.tensor_tensor(
                out=oqks[c][:, :, lo:hi, :].rearrange("p q j (h f) -> p j q h f", h=2),
                in0=pts[c][:, 0, lo:hi, :, :].rearrange("p j q (h f) -> p j q h f", h=2),
                in1=pts[c][:, 1, lo:hi, :, :].rearrange("p j q (h f) -> p j q h f", h=2)[:, :, :, ::-1, :],
                op=ALU.add,
            )

        V, SC, G = nc.vector.tensor_copy, nc.scalar.copy, nc.gpsimd
        table_turns(0, JN, nc.vector)
        table_round(0, JN)
        table_frac(0, JN)
        table_abs(0, JN)
        rest = (JN, J)
        table_turns(*rest, nc.vector)
        w_regroup(2, SC)
        w_regroup(0, V)
        w_regroup(1, V)
        table_scalar(0, JN, 0)
        table_scalar(0, JN, 1)
        w_quantise(cqk, sqk, wgqk)
        transposes(0)
        regroup_tile(0, 0, V)
        regroup_tile(0, 1, SC)
        w_quantise(cv, sv, wgv)
        quantise(0)
        table_round(*rest)
        transposes(1)
        table_scalar(0, JN, 2)
        regroup(1)
        transposes(2)
        regroup(2)
        multiply(0)
        quantise(1)
        table_frac(*rest)
        table_abs(*rest)
        transposes(3)
        regroup(3)
        def finish(i):
            c = i // 2
            lo = (i % 2) * 2
            adds(c, lo, lo + 2, G)
            if lo > 0:
                store(c)
                if c + LEAD < NCH:
                    load_part(c + LEAD, 0, JN)

        LAST = NP - 1
        for i in range(1, LAST - 3):
            multiply(i)
            if i % 2 == 1:
                vcopy(i // 2, 0, JN)
            if i + 5 < NP and i >= 5 and i % 2 == 0 and not (i < 24 and i % 8 == 2):
                sort_words(i + 5, 0)
            transposes(i + AHEAD)
            regroup(i + AHEAD)
            products(i - 1)
            quantise(i + 1)
            finish(i - 1)
            jc, part = divmod(i, 8) if i < 24 else (3, 0)
            if jc + 1 < J // JN and 1 <= part <= 3:
                table_scalar((jc + 1) * JN, (jc + 2) * JN, part - 1)
        multiply(LAST - 3)
        products(LAST - 4)
        quantise(LAST - 2)
        finish(LAST - 4)
        transposes(LAST)
        regroup_tile(LAST, 0, SC)
        regroup_tile(LAST, 1, SC)
        multiply(LAST - 2)
        c = NCH - 2
        vcopy(c, 0, JN)
        store_v(c, 0, JN)
        products(LAST - 3)
        quantise(LAST - 1)
        adds(c, 0, 2, G)
        store_qk(c, 0, 2)
        multiply(LAST - 1)
        vcopy(c + 1, 0, 2)
        store_v(c + 1, 0, 2)
        products(LAST - 2)
        quantise(LAST)
        adds(c, 2, 4, G)
        store_qk(c, 2, 4)
        multiply(LAST)
        products(LAST - 1)
        c = NCH - 1
        vcopy(c, 2, 4)
        store_v(c, 2, 4)
        adds(c, 0, 1, G)
        products(LAST)
        adds(c, 1, 2, nc.vector)
        store_qk(c, 0, 2)
        adds(c, 2, 4, nc.vector)
        store_qk(c, 2, 4)
